import numpy as np
import ml_dtypes


def mxq(x, axis, fmt="e4m3"):
    dtype, down = {"e4m3": (ml_dtypes.float8_e4m3fn, 7), "e5m2": (ml_dtypes.float8_e5m2, 14)}[fmt]
    v = np.moveaxis(np.asarray(x, np.float32).astype(ml_dtypes.bfloat16).astype(np.float64), axis, -1)
    blocks = v.reshape(v.shape[:-1] + (-1, 32))
    amax = np.abs(blocks).max(-1, keepdims=True)
    byte = np.maximum(np.where(amax > 0, np.frexp(amax)[1] - 1 + 127, 0) - down, 1)
    scale = np.exp2(byte - 127.0)
    codes = (blocks / scale).astype(np.float32).astype(dtype).astype(np.float64)
    return np.moveaxis((codes * scale).reshape(v.shape), -1, axis)


WIDE = False


def mx_kscale(k):
    if not WIDE:
        return np.ones(k)
    levels = np.array([18, -18])
    if k % 512:
        return np.exp2(np.random.permutation(np.resize(levels, k // 32))).repeat(32)
    a = np.empty((k // 512, 16))
    for p in range(k // 512):
        a[p, :8] = np.random.permutation(np.resize(levels, 8))
        for g in range(8):
            far = levels[np.abs(levels - a[p, g]) >= 10]
            a[p, g + 8] = far[np.random.randint(len(far))]
    return np.exp2(a.ravel()).repeat(32)


BF16 = ml_dtypes.bfloat16


def bf(x):
    return np.asarray(x, np.float32).astype(BF16)


def f64(x):
    return np.asarray(x).astype(np.float64)


B, S, IQ, OQ, Q = 4, 256, 512, 512, 4


def setup_inputs():
    s = mx_kscale(B * S).reshape(B, S, 1, 1)
    u = mx_kscale(OQ)[:, None]
    sw = 0.5 / np.sqrt(IQ)
    x = bf((np.random.standard_normal((B, S, IQ, Q)) * s).reshape(B, S, IQ * Q))
    wr = bf(np.random.standard_normal((OQ, IQ)) * sw / u)
    wi = bf(np.random.standard_normal((OQ, IQ)) * sw / u)
    wj = bf(np.random.standard_normal((OQ, IQ)) * sw / u)
    wk = bf(np.random.standard_normal((OQ, IQ)) * sw / u)
    bias = bf(np.random.standard_normal(OQ * Q) * 0.3)
    e = np.exp2(np.random.randint(-6, 1, (B, S, 1, 1)))
    g = bf((np.random.standard_normal((B, S, OQ, Q)) * e / s * u).reshape(B, S, OQ * Q))
    return {"x": x, "wr": wr, "wi": wi, "wj": wj, "wk": wk, "bias": bias, "grad_out": g}


def reference(x, wr, wi, wj, wk, bias, grad_out):
    xq = f64(x).reshape(B * S, IQ, Q)
    gq = f64(grad_out).reshape(B * S, OQ, Q)
    g0, g1, g2, g3 = gq[:, :, 0], gq[:, :, 1], gq[:, :, 2], gq[:, :, 3]
    hi = g2 - g0 - g3
    hj = g3 - g0 - g1
    hk = g1 - g0 - g2
    p0 = mxq(g0, 1, "e5m2")
    p1 = mxq(g1, 1, "e5m2")
    p2 = mxq(g2, 1, "e5m2")
    p3 = mxq(g3, 1, "e5m2")
    pi_ = mxq(hi, 1, "e5m2")
    pj_ = mxq(hj, 1, "e5m2")
    pk_ = mxq(hk, 1, "e5m2")
    qr = mxq(f64(wr), 0, "e4m3")
    qi = mxq(f64(wi), 0, "e4m3")
    qj = mxq(f64(wj), 0, "e4m3")
    qk = mxq(f64(wk), 0, "e4m3")
    dxr = (p0 @ qr) + (p1 @ qi) + (p2 @ qj) + (p3 @ qk)
    dxi = (p1 @ qr) + (pi_ @ qi)
    dxj = (p2 @ qr) + (pj_ @ qj)
    dxk = (p3 @ qr) + (pk_ @ qk)
    dx = np.stack([dxr, dxi, dxj, dxk], axis=-1).reshape(B, S, IQ * Q)
    t0 = mxq(g0, 0, "e5m2")
    t1 = mxq(g1, 0, "e5m2")
    t2 = mxq(g2, 0, "e5m2")
    t3 = mxq(g3, 0, "e5m2")
    xr = mxq(xq[:, :, 0], 0, "e4m3")
    xi = mxq(xq[:, :, 1], 0, "e4m3")
    xj = mxq(xq[:, :, 2], 0, "e4m3")
    xk = mxq(xq[:, :, 3], 0, "e4m3")
    dwr = (t0.T @ xr) + (t1.T @ xi) + (t2.T @ xj) + (t3.T @ xk)
    return dx, dwr

@@ -1,0 +1,313 @@
+from contextlib import ExitStack
+
+import concourse.mybir as mybir
+from concourse.masks import make_identity
+
+F32 = mybir.dt.float32
+BF16 = mybir.dt.bfloat16
+U32 = mybir.dt.uint32
+U8 = mybir.dt.uint8
+E4M3 = mybir.dt.float8_e4m3fn_x4
+E5M2 = mybir.dt.float8_e5m2_x4
+ADD = mybir.AluOpType.add
+SUB = mybir.AluOpType.subtract
+
+P = 128
+PACK = 4
+COMP = 4
+TOKENS = 1024
+QUAT = 512
+WIDTH = QUAT * COMP
+PASSES = TOKENS // (P * PACK)
+TILES = PASSES * PACK
+QTILES = QUAT // P
+
+FLOPS = 2 * TOKENS * QUAT * QUAT * 14
+BYTES = 2 * TOKENS * WIDTH * 2 + 4 * QUAT * QUAT * 2 + TOKENS * WIDTH * 4 + QUAT * QUAT * 4
+
+SCALAR_CHUNKS = (2, 1, 1, 2, 1, 2, 1, 0)
+VECTOR_CHUNKS = (1, 1, 1, 0, 1, 1, 1, 0)
+
+
+def tile_quaternionlinear_pa_v_kernel(tc, x, wr, wi, wj, wk, bias, grad_out, out_0, out_1):
+    nc = tc.nc
+    x_rows = x.rearrange("b s w -> (b s) w").rearrange("(g p j) w -> g p j w", g=PASSES, j=PACK)
+    g_rows = grad_out.rearrange("b s w -> (b s) w").rearrange("(g p j) w -> g p j w", g=PASSES, j=PACK)
+    dx_rows = out_0.rearrange("b s w -> (b s) w").rearrange("(g p j) w -> g p j w", g=PASSES, j=PACK)
+    weights = (wr, wi, wj, wk)
+
+    with ExitStack() as ctx:
+        keep = ctx.enter_context(tc.tile_pool(name="keep", bufs=1))
+        work = ctx.enter_context(tc.tile_pool(name="work", bufs=2))
+        psum = ctx.enter_context(tc.psum_pool(name="psum", bufs=4))
+        ctx.enter_context(tc.manual_schedule())
+
+        ident = keep.tile([P, P], F32, name="ident")
+        make_identity(nc, ident[:])
+
+        g_raw = [keep.tile([P, PACK * WIDTH], BF16, name="g_raw%d" % g, align_bytes=64) for g in range(PASSES)]
+        x_raw = [keep.tile([P, PACK * QUAT], BF16, name="x_raw%d" % n, align_bytes=64) for n in range(PASSES * QTILES)]
+        w_raw = [keep.tile([P, PACK * QUAT], BF16, name="w_raw%d" % c, align_bytes=64) for c in range(COMP)]
+        w_codes = [keep.tile([P, QUAT], U32, name="w_codes%d" % c, align_bytes=64) for c in range(COMP)]
+        w_scales = [keep.tile([P, QUAT], U8, name="w_scales%d" % c, align_bytes=64) for c in range(COMP)]
+        x_codes = [keep.tile([P, WIDTH], U32, name="x_codes%d" % g, align_bytes=64) for g in range(PASSES)]
+        x_scales = [keep.tile([P, WIDTH], U8, name="x_scales%d" % g, align_bytes=64) for g in range(PASSES)]
+
+        def load_g(k):
+            g, j = divmod(k, PACK)
+            nc.sync.dma_start(out=g_raw[g][:, j * WIDTH:(j + 1) * WIDTH], in_=g_rows[g, :, j, :])
+
+        def load_w(c):
+            nc.sync.dma_start(out=w_raw[c][:], in_=weights[c].rearrange("(p j) i -> p (j i)", j=PACK))
+
+        def load_x(n):
+            g, q = divmod(n, QTILES)
+            nc.sync.dma_start(out=x_raw[n][:].rearrange("p (j w) -> p j w", j=PACK),
+                              in_=x_rows[g, :, :, q * QUAT:(q + 1) * QUAT])
+
+        def copy_on(engine, out, in_):
+            if engine == "vector":
+                nc.vector.tensor_copy(out=out, in_=in_)
+            else:
+                nc.scalar.copy(out=out, in_=in_)
+
+        grouped = {}
+
+        def group_weight(c, engine):
+            t = work.tile([P, WIDTH], BF16, name="grp_" + engine, tag="grp_" + engine, bufs=3, align_bytes=64)
+            copy_on(engine,
+                    t[:].rearrange("p (b i j) -> p b j i", i=4, j=PACK),
+                    w_raw[c][:].rearrange("p (j b i) -> p b j i", j=PACK, i=4))
+            grouped[("w", c)] = t
+
+        def quantize_weight(c):
+            nc.vector.quantize_mx(out=w_codes[c][:].bitcast(E4M3), scales=w_scales[c][:], in_=grouped[("w", c)][:])
+
+        def chunk_place(n):
+            if n < PASSES * QTILES:
+                return divmod(n, QTILES)
+            q, g = divmod(n - PASSES * QTILES, PASSES)
+            return g, q
+
+        def group_chunk(n, engine):
+            g, q = chunk_place(n)
+            t = work.tile([P, WIDTH], BF16, name="grp_" + engine, tag="grp_" + engine, bufs=3, align_bytes=64)
+            if n < PASSES * QTILES:
+                src = x_raw[n][:].rearrange("p (j b i c) -> p b c i j", j=PACK, i=2, c=COMP)
+            else:
+                src = g_raw[g][:].rearrange("p (j b i c) -> p b c i j", j=PACK, i=2, c=COMP)[:, q * 64:(q + 1) * 64]
+            copy_on(engine, t[:].rearrange("p (c b i j) -> p b c i j", c=COMP, i=2, j=PACK), src)
+            grouped[n] = t
+
+        gtok = {}
+
+        def quantize_chunk(n):
+            g, q = chunk_place(n)
+            t = grouped[n]
+            if n < PASSES * QTILES:
+                for c in range(COMP):
+                    cols = slice(c * QUAT + q * P, c * QUAT + (q + 1) * P)
+                    nc.vector.quantize_mx(out=x_codes[g][:, cols].bitcast(E4M3), scales=x_scales[g][:, cols],
+                                          in_=t[:, c * QUAT:(c + 1) * QUAT])
+            else:
+                codes = work.tile([P, QUAT], U32, name="gtok_codes", tag="gtok_codes", bufs=4, align_bytes=64)
+                scales = work.tile([P, QUAT], U8, name="gtok_scales", tag="gtok_scales", bufs=4, align_bytes=64)
+                nc.vector.quantize_mx(out=codes[:].bitcast(E5M2), scales=scales[:], in_=t[:])
+                gtok[(g, q)] = (codes, scales)
+
+        banks = {}
+
+        def transpose_tile(k):
+            g, j = divmod(k, PACK)
+            words = g_raw[g][:].bitcast(F32)
+            row = WIDTH // 2
+            for half in range(2):
+                bank = psum.tile([P, PACK * P], F32, name="turned", tag="turned")
+                for t in range(PACK):
+                    nc.tensor.transpose(bank[:, t * P:(t + 1) * P],
+                                        words[:, j * row + 2 * t + half:(j + 1) * row:8], ident[:])
+                banks[(k, half)] = bank[:].bitcast(BF16).rearrange("m (t p e) -> m e p t", t=PACK, e=2)
+
+        g_feat = {}
+
+        def copy_turned(k):
+            t = work.tile([P, WIDTH], BF16, name="g_feat", tag="g_feat", align_bytes=64)
+            for half in range(2):
+                nc.scalar.copy(out=t[:, half * 2 * QUAT:(half + 1) * 2 * QUAT].rearrange("m (e p t) -> m e p t", e=2, t=PACK),
+                               in_=banks[(k, half)])
+            g_feat[k] = t
+
+        gq = {}
+        hq = {}
+        h_feat = {}
+
+        def quantize_g(k):
+            codes = work.tile([P, QUAT], U32, name="g_codes", tag="g_codes", align_bytes=64)
+            scales = work.tile([P, QUAT], U8, name="g_scales", tag="g_scales", align_bytes=64)
+            nc.vector.quantize_mx(out=codes[:].bitcast(E5M2), scales=scales[:], in_=g_feat[k][:])
+            gq[k] = (codes, scales)
+
+        def combine(k):
+            sums = work.tile([P, 3 * QUAT], F32, name="sums", tag="sums", bufs=1)
+            h = work.tile([P, 3 * QUAT], BF16, name="h_feat", tag="h_feat", align_bytes=64)
+            g0 = g_feat[k][:, 0:QUAT].rearrange("m (p t) -> m p t", t=PACK)
+
+            def comp(c):
+                return banks[(k, c // 2)][:, c % 2]
+
+            def part(tile, s):
+                return tile[:, s * QUAT:(s + 1) * QUAT].rearrange("m (p t) -> m p t", t=PACK)
+
+            nc.vector.tensor_tensor(out=part(sums, 1), in0=comp(2), in1=g0, op=ADD)
+            nc.vector.tensor_tensor(out=part(sums, 0), in0=comp(1), in1=g0, op=ADD)
+            nc.vector.tensor_tensor(out=part(h, 0), in0=comp(1), in1=part(sums, 1), op=SUB)
+            nc.vector.tensor_tensor(out=part(sums, 2), in0=comp(3), in1=g0, op=ADD)
+            nc.vector.tensor_tensor(out=part(h, 1), in0=comp(3), in1=part(sums, 0), op=SUB)
+            nc.vector.tensor_tensor(out=part(h, 2), in0=comp(2), in1=part(sums, 2), op=SUB)
+            h_feat[k] = h
+
+        def quantize_h(k):
+            codes = work.tile([P, 3 * P], U32, name="h_codes", tag="h_codes", align_bytes=64)
+            scales = work.tile([P, 3 * P], U8, name="h_scales", tag="h_scales", align_bytes=64)
+            h = h_feat[k]
+            nc.vector.quantize_mx(out=codes[:, 0:2 * P].bitcast(E5M2), scales=scales[:, 0:2 * P], in_=h[:, 0:2 * QUAT])
+            nc.vector.quantize_mx(out=codes[:, 2 * P:3 * P].bitcast(E5M2), scales=scales[:, 2 * P:3 * P],
+                                  in_=h[:, 2 * QUAT:3 * QUAT])
+            hq[k] = (codes, scales)
+
+        def mx(acc, left, s, right_codes, right_scales, start, stop):
+            codes, scales = left
+            cols = slice(s * P, (s + 1) * P)
+            nc.tensor.matmul_mx(out=acc[:], lhsT=codes[:, cols].bitcast(E5M2), lhsT_scale=scales[:, cols],
+                                rhs=right_codes.bitcast(E4M3), rhs_scale=right_scales, start=start, stop=stop)
+
+        accs = {}
+
+        def multiply_real(k):
+            acc = psum.tile([P, QUAT], F32, name="acc", tag="acc")
+            for c in range(COMP):
+                mx(acc, gq[k], c, w_codes[c][:], w_scales[c][:], c == 0, c == COMP - 1)
+            accs[(k, 0)] = acc
+
+        def multiply_imag(k):
+            for c in (3, 2, 1):
+                acc = psum.tile([P, QUAT], F32, name="acc", tag="acc")
+                mx(acc, gq[k], c, w_codes[0][:], w_scales[0][:], True, False)
+                mx(acc, hq[k], 3 - c, w_codes[c][:], w_scales[c][:], False, True)
+                accs[(k, c)] = acc
+
+        def multiply_weight_grad(q):
+            acc = psum.tile([P, QUAT], F32, name="acc", tag="acc")
+            for g in range(PASSES):
+                for c in range(COMP):
+                    cols = slice(c * QUAT, (c + 1) * QUAT)
+                    mx(acc, gtok[(g, q)], c, x_codes[g][:, cols], x_scales[g][:, cols],
+                       g == 0 and c == 0, g == PASSES - 1 and c == COMP - 1)
+            accs[("w", q)] = acc
+
+        planar = {}
+
+        def drain(k, c):
+            if c == 0:
+                planar[k] = work.tile([P, WIDTH], F32, name="planar", tag="planar")
+            nc.scalar.copy(out=planar[k][:, c * QUAT:(c + 1) * QUAT], in_=accs[(k, c)][:])
+
+        def drain_weight_grad(q):
+            t = work.tile([P, QUAT], F32, name="dw", tag="dw")
+            nc.scalar.copy(out=t[:], in_=accs[("w", q)][:])
+            nc.sync.dma_start(out=out_1[q * P:(q + 1) * P, :], in_=t[:])
+
+        def weave_and_store(k, parts):
+            g, j = divmod(k, PACK)
+            t = work.tile([P, WIDTH], F32, name="woven", tag="woven", bufs=3)
+            dst = t[:].rearrange("p (b i c) -> p b c i", i=4, c=COMP)
+            src = planar[k][:].rearrange("p (c b i) -> p b c i", c=COMP, i=4)
+            nb = P // parts
+            w = WIDTH // parts
+            for s in range(parts):
+                nc.vector.tensor_copy(out=dst[:, s * nb:(s + 1) * nb], in_=src[:, s * nb:(s + 1) * nb])
+                nc.sync.dma_start(out=dx_rows[g, :, j, s * w:(s + 1) * w], in_=t[:, s * w:(s + 1) * w])
+
+        load_w(0)
+        load_w(1)
+        load_g(0)
+        load_w(2)
+        load_g(1)
+        load_w(3)
+        load_x(0)
+        load_x(1)
+        load_x(2)
+        load_g(2)
+        load_x(3)
+        load_g(3)
+        load_x(4)
+        load_x(5)
+        load_g(4)
+        load_x(6)
+        load_x(7)
+        for k in range(5, TILES):
+            load_g(k)
+
+        group_weight(0, "vector")
+        group_weight(1, "scalar")
+        transpose_tile(0)
+        transpose_tile(1)
+        copy_turned(0)
+        group_weight(2, "vector")
+        quantize_weight(0)
+        quantize_weight(1)
+        quantize_weight(2)
+        group_weight(3, "scalar")
+
+        nxt = 0
+        waiting = []
+        next_q = 0
+        for k in range(TILES):
+            quantize_g(k)
+            if k > 0:
+                multiply_real(k)
+                for c in (3, 2, 1):
+                    drain(k - 1, c)
+            weight_grad_now = (0, next_q) in gtok and (1, next_q) in gtok
+            if weight_grad_now:
+                multiply_weight_grad(next_q)
+            combine(k)
+            if k == 0:
+                quantize_weight(3)
+                multiply_real(0)
+            if k + 2 < TILES:
+                transpose_tile(k + 2)
+            if k + 1 < TILES:
+                copy_turned(k + 1)
+            drain(k, 0)
+            if weight_grad_now:
+                drain_weight_grad(next_q)
+                next_q = next_q + 1
+            mine = []
+            for s in range(VECTOR_CHUNKS[k]):
+                group_chunk(nxt, "vector")
+                mine.append(nxt)
+                nxt = nxt + 1
+            theirs = []
+            for s in range(SCALAR_CHUNKS[k]):
+                group_chunk(nxt, "scalar")
+                theirs.append(nxt)
+                nxt = nxt + 1
+            if not mine and waiting:
+                quantize_chunk(waiting[0])
+                waiting = waiting[1:]
+            quantize_h(k)
+            multiply_imag(k)
+            for n in waiting + mine:
+                quantize_chunk(n)
+            waiting = theirs
+            if k > 0:
+                weave_and_store(k - 1, 1)
+
+        last = TILES - 1
+        for c in (3, 2, 1):
+            drain(last, c)
+        for q in range(next_q, QTILES):
+            multiply_weight_grad(q)
+            drain_weight_grad(q)
+        weave_and_store(last, 2)

@@ -11,6 +11,7 @@ E4M3 = mybir.dt.float8_e4m3fn_x4
 E5M2 = mybir.dt.float8_e5m2_x4
 ADD = mybir.AluOpType.add
 SUB = mybir.AluOpType.subtract
+MULT = mybir.AluOpType.mult
 
 P = 128
 PACK = 4
@@ -24,9 +25,6 @@ QTILES = QUAT // P
 
 FLOPS = 2 * TOKENS * QUAT * QUAT * 14
 BYTES = 2 * TOKENS * WIDTH * 2 + 4 * QUAT * QUAT * 2 + TOKENS * WIDTH * 4 + QUAT * QUAT * 4
-
-SCALAR_CHUNKS = (2, 1, 1, 2, 1, 2, 1, 0)
-VECTOR_CHUNKS = (1, 1, 1, 0, 1, 1, 1, 0)
 
 
 def tile_quaternionlinear_pa_v_kernel(tc, x, wr, wi, wj, wk, bias, grad_out, out_0, out_1):
@@ -73,8 +71,12 @@ def tile_quaternionlinear_pa_v_kernel(tc, x, wr, wi, wj, wk, bias, grad_out, out
 
         grouped = {}
 
-        def group_weight(c, engine):
-            t = work.tile([P, WIDTH], BF16, name="grp_" + engine, tag="grp_" + engine, bufs=3, align_bytes=64)
+        def group_tile(owner):
+            depth = {"vector": 2, "scalar": 2, "gpsimd": 1}[owner]
+            return work.tile([P, WIDTH], BF16, name="grp_" + owner, tag="grp_" + owner, bufs=depth, align_bytes=64)
+
+        def group_weight(c, engine, owner):
+            t = group_tile(owner)
             copy_on(engine,
                     t[:].rearrange("p (b i j) -> p b j i", i=4, j=PACK),
                     w_raw[c][:].rearrange("p (j b i) -> p b j i", j=PACK, i=4))
@@ -91,12 +93,18 @@ def tile_quaternionlinear_pa_v_kernel(tc, x, wr, wi, wj, wk, bias, grad_out, out
 
         def group_chunk(n, engine):
             g, q = chunk_place(n)
-            t = work.tile([P, WIDTH], BF16, name="grp_" + engine, tag="grp_" + engine, bufs=3, align_bytes=64)
+            t = group_tile(engine)
             if n < PASSES * QTILES:
-                src = x_raw[n][:].rearrange("p (j b i c) -> p b c i j", j=PACK, i=2, c=COMP)
+                raw = x_raw[n][:].rearrange("p (j w) -> p j w", j=PACK)
             else:
-                src = g_raw[g][:].rearrange("p (j b i c) -> p b c i j", j=PACK, i=2, c=COMP)[:, q * 64:(q + 1) * 64]
-            copy_on(engine, t[:].rearrange("p (c b i j) -> p b c i j", c=COMP, i=2, j=PACK), src)
+                raw = g_raw[g][:].rearrange("p (j w) -> p j w", j=PACK)[:, :, q * QUAT:(q + 1) * QUAT]
+            if engine == "gpsimd":
+                nc.gpsimd.tensor_scalar(out=t[:].rearrange("p (c i j) -> p i c j", c=COMP, j=PACK),
+                                        in0=raw.rearrange("p j (i c) -> p i c j", c=COMP),
+                                        scalar1=1.0, scalar2=0.0, op0=MULT, op1=ADD)
+            else:
+                copy_on(engine, t[:].rearrange("p (c b i j) -> p b c i j", c=COMP, i=2, j=PACK),
+                        raw.rearrange("p j (b i c) -> p b c i j", i=2, c=COMP))
             grouped[n] = t
 
         gtok = {}
@@ -189,125 +197,129 @@ def tile_quaternionlinear_pa_v_kernel(tc, x, wr, wi, wj, wk, bias, grad_out, out
                 mx(acc, gq[k], c, w_codes[c][:], w_scales[c][:], c == 0, c == COMP - 1)
             accs[(k, 0)] = acc
 
-        def multiply_imag(k):
-            for c in (3, 2, 1):
-                acc = psum.tile([P, QUAT], F32, name="acc", tag="acc")
-                mx(acc, gq[k], c, w_codes[0][:], w_scales[0][:], True, False)
-                mx(acc, hq[k], 3 - c, w_codes[c][:], w_scales[c][:], False, True)
-                accs[(k, c)] = acc
-
-        def multiply_weight_grad(q):
+        def open_imag(k, c):
             acc = psum.tile([P, QUAT], F32, name="acc", tag="acc")
-            for g in range(PASSES):
-                for c in range(COMP):
-                    cols = slice(c * QUAT, (c + 1) * QUAT)
-                    mx(acc, gtok[(g, q)], c, x_codes[g][:, cols], x_scales[g][:, cols],
-                       g == 0 and c == 0, g == PASSES - 1 and c == COMP - 1)
-            accs[("w", q)] = acc
+            mx(acc, gq[k], c, w_codes[0][:], w_scales[0][:], True, False)
+            accs[(k, c)] = acc
+
+        def close_imag(k, c):
+            mx(accs[(k, c)], hq[k], 3 - c, w_codes[c][:], w_scales[c][:], False, True)
+
+        def multiply_weight_grad(q, g):
+            if g == 0:
+                tag = "acc" if q < 2 else "turned"
+                accs[("w", q)] = psum.tile([P, QUAT], F32, name=tag, tag=tag)
+            for c in range(COMP):
+                cols = slice(c * QUAT, (c + 1) * QUAT)
+                mx(accs[("w", q)], gtok[(g, q)], c, x_codes[g][:, cols], x_scales[g][:, cols],
+                   g == 0 and c == 0, g == PASSES - 1 and c == COMP - 1)
 
         planar = {}
 
-        def drain(k, c):
-            if c == 0:
+        def drain(k, c, engine):
+            if k not in planar:
                 planar[k] = work.tile([P, WIDTH], F32, name="planar", tag="planar")
-            nc.scalar.copy(out=planar[k][:, c * QUAT:(c + 1) * QUAT], in_=accs[(k, c)][:])
+            copy_on(engine, planar[k][:, c * QUAT:(c + 1) * QUAT], accs[(k, c)][:])
 
         def drain_weight_grad(q):
             t = work.tile([P, QUAT], F32, name="dw", tag="dw")
             nc.scalar.copy(out=t[:], in_=accs[("w", q)][:])
             nc.sync.dma_start(out=out_1[q * P:(q + 1) * P, :], in_=t[:])
 
-        def weave_and_store(k, parts):
+        def weave_and_store(k, engines):
             g, j = divmod(k, PACK)
             t = work.tile([P, WIDTH], F32, name="woven", tag="woven", bufs=3)
             dst = t[:].rearrange("p (b i c) -> p b c i", i=4, c=COMP)
             src = planar[k][:].rearrange("p (c b i) -> p b c i", c=COMP, i=4)
-            nb = P // parts
-            w = WIDTH // parts
-            for s in range(parts):
-                nc.vector.tensor_copy(out=dst[:, s * nb:(s + 1) * nb], in_=src[:, s * nb:(s + 1) * nb])
+            nb = P // len(engines)
+            w = WIDTH // len(engines)
+            for s, engine in enumerate(engines):
+                copy_on(engine, dst[:, s * nb:(s + 1) * nb], src[:, s * nb:(s + 1) * nb])
                 nc.sync.dma_start(out=dx_rows[g, :, j, s * w:(s + 1) * w], in_=t[:, s * w:(s + 1) * w])
 
         load_w(0)
-        load_w(1)
         load_g(0)
+        load_w(1)
         load_w(2)
-        load_g(1)
         load_w(3)
+        load_g(1)
         load_x(0)
         load_x(1)
         load_x(2)
-        load_g(2)
-        load_x(3)
-        load_g(3)
-        load_x(4)
-        load_x(5)
-        load_g(4)
-        load_x(6)
-        load_x(7)
-        for k in range(5, TILES):
+        for k in range(2, TILES):
             load_g(k)
+            for n in range(2 * k - 1, min(2 * k + 1, PASSES * QTILES)):
+                load_x(n)
 
-        group_weight(0, "vector")
-        group_weight(1, "scalar")
-        transpose_tile(0)
-        transpose_tile(1)
-        copy_turned(0)
-        group_weight(2, "vector")
+        group_weight(0, "vector", "vector")
         quantize_weight(0)
+        transpose_tile(0)
+        copy_turned(0)
+        group_weight(1, "vector", "vector")
+        group_weight(2, "vector", "gpsimd")
         quantize_weight(1)
-        quantize_weight(2)
-        group_weight(3, "scalar")
+        group_weight(3, "scalar", "scalar")
+        transpose_tile(1)
 
-        nxt = 0
-        waiting = []
-        next_q = 0
+        last = TILES - 1
+        imag = (3, 2, 1)
         for k in range(TILES):
+            by_gpsimd = 2 * k + 1 if k > 0 else 0
+            by_scalar = 2 * k + 2 if k > 0 else 1
+            gpsimd_before = 2 * k - 1 if k > 1 else 0
+            scalar_before = 2 * k if k > 1 else 1
+            q = k - 5
             quantize_g(k)
-            if k > 0:
+            if k == 0:
+                quantize_weight(2)
+            else:
                 multiply_real(k)
-                for c in (3, 2, 1):
-                    drain(k - 1, c)
-            weight_grad_now = (0, next_q) in gtok and (1, next_q) in gtok
-            if weight_grad_now:
-                multiply_weight_grad(next_q)
+                quantize_chunk(gpsimd_before)
+                for c in imag:
+                    drain(k - 1, c, "scalar")
+            group_chunk(by_gpsimd, "gpsimd")
+            if q >= 0:
+                for g in range(PASSES):
+                    multiply_weight_grad(q, g)
+            if k == last:
+                for c in imag:
+                    open_imag(k, c)
             combine(k)
             if k == 0:
                 quantize_weight(3)
                 multiply_real(0)
             if k + 2 < TILES:
                 transpose_tile(k + 2)
-            if k + 1 < TILES:
+            if k < last:
                 copy_turned(k + 1)
-            drain(k, 0)
-            if weight_grad_now:
-                drain_weight_grad(next_q)
-                next_q = next_q + 1
-            mine = []
-            for s in range(VECTOR_CHUNKS[k]):
-                group_chunk(nxt, "vector")
-                mine.append(nxt)
-                nxt = nxt + 1
-            theirs = []
-            for s in range(SCALAR_CHUNKS[k]):
-                group_chunk(nxt, "scalar")
-                theirs.append(nxt)
-                nxt = nxt + 1
-            if not mine and waiting:
-                quantize_chunk(waiting[0])
-                waiting = waiting[1:]
+            else:
+                weave_and_store(k - 1, ["scalar"])
+            drain(k, 0, "scalar")
+            if q >= 0:
+                drain_weight_grad(q)
+            if k < last:
+                group_chunk(by_scalar, "scalar")
+            if k == 0:
+                group_chunk(2, "vector")
+            elif k < last:
+                weave_and_store(k - 1, ["vector"])
+            else:
+                quantize_chunk(scalar_before)
             quantize_h(k)
-            multiply_imag(k)
-            for n in waiting + mine:
-                quantize_chunk(n)
-            waiting = theirs
-            if k > 0:
-                weave_and_store(k - 1, 1)
+            for c in imag:
+                if k < last:
+                    open_imag(k, c)
+                close_imag(k, c)
+            if k == 0:
+                quantize_chunk(2)
+            elif k < last:
+                quantize_chunk(scalar_before)
 
-        last = TILES - 1
-        for c in (3, 2, 1):
-            drain(last, c)
-        for q in range(next_q, QTILES):
-            multiply_weight_grad(q)
-            drain_weight_grad(q)
-        weave_and_store(last, 2)
+        quantize_chunk(2 * last + 1)
+        for g in range(PASSES):
+            multiply_weight_grad(QTILES - 1, g)
+        drain(last, 3, "scalar")
+        drain(last, 2, "vector")
+        drain(last, 1, "scalar")
+        weave_and_store(last, ["vector", "vector", "scalar", "vector"])
+        drain_weight_grad(QTILES - 1)

@@ -66,13 +66,15 @@ def tile_quaternionlinear_pa_v_kernel(tc, x, wr, wi, wj, wk, bias, grad_out, out
         def copy_on(engine, out, in_):
             if engine == "vector":
                 nc.vector.tensor_copy(out=out, in_=in_)
+            elif engine == "gpsimd":
+                nc.gpsimd.tensor_scalar(out=out, in0=in_, scalar1=1.0, scalar2=0.0, op0=MULT, op1=ADD)
             else:
                 nc.scalar.copy(out=out, in_=in_)
 
         grouped = {}
 
         def group_tile(owner):
-            depth = {"vector": 2, "scalar": 2, "gpsimd": 1}[owner]
+            depth = {"vector": 2, "scalar": 3, "gpsimd": 1}[owner]
             return work.tile([P, WIDTH], BF16, name="grp_" + owner, tag="grp_" + owner, bufs=depth, align_bytes=64)
 
         def group_weight(c, engine, owner):
@@ -103,8 +105,8 @@ def tile_quaternionlinear_pa_v_kernel(tc, x, wr, wi, wj, wk, bias, grad_out, out
                                         in0=raw.rearrange("p j (i c) -> p i c j", c=COMP),
                                         scalar1=1.0, scalar2=0.0, op0=MULT, op1=ADD)
             else:
-                copy_on(engine, t[:].rearrange("p (c b i j) -> p b c i j", c=COMP, i=2, j=PACK),
-                        raw.rearrange("p j (b i c) -> p b c i j", i=2, c=COMP))
+                copy_on(engine, t[:].rearrange("p (c b i j) -> p b j i c", c=COMP, i=2, j=PACK),
+                        raw.rearrange("p j (b i c) -> p b j i c", i=2, c=COMP))
             grouped[n] = t
 
         gtok = {}
@@ -159,19 +161,19 @@ def tile_quaternionlinear_pa_v_kernel(tc, x, wr, wi, wj, wk, bias, grad_out, out
             sums = work.tile([P, 3 * QUAT], F32, name="sums", tag="sums", bufs=1)
             h = work.tile([P, 3 * QUAT], BF16, name="h_feat", tag="h_feat", align_bytes=64)
             g0 = g_feat[k][:, 0:QUAT].rearrange("m (p t) -> m p t", t=PACK)
+            g1 = banks[(k, 0)][:, 1]
+            g23 = banks[(k, 1)]
 
-            def comp(c):
-                return banks[(k, c // 2)][:, c % 2]
-
-            def part(tile, s):
+            def one(tile, s):
                 return tile[:, s * QUAT:(s + 1) * QUAT].rearrange("m (p t) -> m p t", t=PACK)
 
-            nc.vector.tensor_tensor(out=part(sums, 1), in0=comp(2), in1=g0, op=ADD)
-            nc.vector.tensor_tensor(out=part(sums, 0), in0=comp(1), in1=g0, op=ADD)
-            nc.vector.tensor_tensor(out=part(h, 0), in0=comp(1), in1=part(sums, 1), op=SUB)
-            nc.vector.tensor_tensor(out=part(sums, 2), in0=comp(3), in1=g0, op=ADD)
-            nc.vector.tensor_tensor(out=part(h, 1), in0=comp(3), in1=part(sums, 0), op=SUB)
-            nc.vector.tensor_tensor(out=part(h, 2), in0=comp(2), in1=part(sums, 2), op=SUB)
+            def two(tile, s):
+                return tile[:, s * QUAT:(s + 2) * QUAT].rearrange("m (e p t) -> m e p t", e=2, t=PACK)
+
+            nc.vector.tensor_tensor(out=two(sums, 0), in0=g23, in1=g0.unsqueeze(1).to_broadcast([P, 2, P, PACK]), op=ADD)
+            nc.vector.tensor_tensor(out=one(sums, 2), in0=g1, in1=g0, op=ADD)
+            nc.vector.tensor_tensor(out=one(h, 0), in0=g1, in1=one(sums, 0), op=SUB)
+            nc.vector.tensor_tensor(out=two(h, 1), in0=g23, in1=two(sums, 1), op=SUB)
             h_feat[k] = h
 
         def quantize_h(k):
@@ -203,7 +205,7 @@ def tile_quaternionlinear_pa_v_kernel(tc, x, wr, wi, wj, wk, bias, grad_out, out
             accs[(k, c)] = acc
 
         def close_imag(k, c):
-            mx(accs[(k, c)], hq[k], 3 - c, w_codes[c][:], w_scales[c][:], False, True)
+            mx(accs[(k, c)], hq[k], c % 3, w_codes[c][:], w_scales[c][:], False, True)
 
         def multiply_weight_grad(q, g):
             if g == 0:
@@ -221,9 +223,9 @@ def tile_quaternionlinear_pa_v_kernel(tc, x, wr, wi, wj, wk, bias, grad_out, out
                 planar[k] = work.tile([P, WIDTH], F32, name="planar", tag="planar")
             copy_on(engine, planar[k][:, c * QUAT:(c + 1) * QUAT], accs[(k, c)][:])
 
-        def drain_weight_grad(q):
+        def drain_weight_grad(q, engine):
             t = work.tile([P, QUAT], F32, name="dw", tag="dw")
-            nc.scalar.copy(out=t[:], in_=accs[("w", q)][:])
+            copy_on(engine, t[:], accs[("w", q)][:])
             nc.sync.dma_start(out=out_1[q * P:(q + 1) * P, :], in_=t[:])
 
         def weave_and_store(k, engines):
@@ -238,46 +240,45 @@ def tile_quaternionlinear_pa_v_kernel(tc, x, wr, wi, wj, wk, bias, grad_out, out
                 nc.sync.dma_start(out=dx_rows[g, :, j, s * w:(s + 1) * w], in_=t[:, s * w:(s + 1) * w])
 
         load_w(0)
-        load_g(0)
         load_w(1)
+        load_g(0)
         load_w(2)
         load_w(3)
         load_g(1)
-        load_x(0)
-        load_x(1)
-        load_x(2)
+        for n in range(3):
+            load_x(n)
         for k in range(2, TILES):
             load_g(k)
             for n in range(2 * k - 1, min(2 * k + 1, PASSES * QTILES)):
                 load_x(n)
 
         group_weight(0, "vector", "vector")
+        group_weight(1, "scalar", "scalar")
         quantize_weight(0)
         transpose_tile(0)
         copy_turned(0)
-        group_weight(1, "vector", "vector")
         group_weight(2, "vector", "gpsimd")
         quantize_weight(1)
-        group_weight(3, "scalar", "scalar")
+        group_weight(3, "vector", "vector")
         transpose_tile(1)
 
         last = TILES - 1
         imag = (3, 2, 1)
+        scalar_chunks = [[1, 2], [4], [6], [8], [10], [12], [], [14]]
         for k in range(TILES):
-            by_gpsimd = 2 * k + 1 if k > 0 else 0
-            by_scalar = 2 * k + 2 if k > 0 else 1
-            gpsimd_before = 2 * k - 1 if k > 1 else 0
-            scalar_before = 2 * k if k > 1 else 1
             q = k - 5
             quantize_g(k)
             if k == 0:
+                quantize_weight(3)
                 quantize_weight(2)
+                multiply_real(0)
             else:
                 multiply_real(k)
-                quantize_chunk(gpsimd_before)
                 for c in imag:
                     drain(k - 1, c, "scalar")
-            group_chunk(by_gpsimd, "gpsimd")
+                pass
+                quantize_chunk(2 * k - 1 if k > 1 else 0)
+            group_chunk(2 * k + 1 if k > 0 else 0, "gpsimd")
             if q >= 0:
                 for g in range(PASSES):
                     multiply_weight_grad(q, g)
@@ -285,41 +286,41 @@ def tile_quaternionlinear_pa_v_kernel(tc, x, wr, wi, wj, wk, bias, grad_out, out
                 for c in imag:
                     open_imag(k, c)
             combine(k)
-            if k == 0:
-                quantize_weight(3)
-                multiply_real(0)
+            pass
             if k + 2 < TILES:
                 transpose_tile(k + 2)
             if k < last:
                 copy_turned(k + 1)
-            else:
-                weave_and_store(k - 1, ["scalar"])
+            if k == last and False:
+                quantize_chunk(15)
+                pass
+            if 0 < k < TILES and not (k == last and False):
+                weave_and_store(k - 1, ["vector"] if k < last else ["vector", "vector"])
+            for n in scalar_chunks[k]:
+                group_chunk(n, "scalar")
             drain(k, 0, "scalar")
             if q >= 0:
-                drain_weight_grad(q)
-            if k < last:
-                group_chunk(by_scalar, "scalar")
-            if k == 0:
-                group_chunk(2, "vector")
-            elif k < last:
-                weave_and_store(k - 1, ["vector"])
-            else:
-                quantize_chunk(scalar_before)
+                drain_weight_grad(q, "scalar")
+            if k == last - 1 and False:
+                for c in imag:
+                    open_imag(k, c)
             quantize_h(k)
             for c in imag:
-                if k < last:
+                if k < last - 0:
                     open_imag(k, c)
                 close_imag(k, c)
-            if k == 0:
-                quantize_chunk(2)
-            elif k < last:
-                quantize_chunk(scalar_before)
+            if k == last and False:
+                weave_and_store(k - 1, ["vector", "vector"])
+            if k > 0:
+                for n in scalar_chunks[k - 1]:
+                    quantize_chunk(n)
 
-        quantize_chunk(2 * last + 1)
-        for g in range(PASSES):
-            multiply_weight_grad(QTILES - 1, g)
+        quantize_chunk(14)
+        multiply_weight_grad(3, 0)
+        quantize_chunk(15)
+        multiply_weight_grad(3, 1)
         drain(last, 3, "scalar")
         drain(last, 2, "vector")
         drain(last, 1, "scalar")
         weave_and_store(last, ["vector", "vector", "scalar", "vector"])
-        drain_weight_grad(QTILES - 1)
+        drain_weight_grad(QTILES - 1, "scalar")

@@ -19,19 +19,26 @@ COMP = 4
 TOKENS = 1024
 QUAT = 512
 WIDTH = QUAT * COMP
+WORDS = WIDTH // 2
 PASSES = TOKENS // (P * PACK)
 TILES = PASSES * PACK
 QTILES = QUAT // P
+X_CHUNKS = PASSES * QTILES
+IMAG = (3, 2, 1)
 
 FLOPS = 2 * TOKENS * QUAT * QUAT * 14
 BYTES = 2 * TOKENS * WIDTH * 2 + 4 * QUAT * QUAT * 2 + TOKENS * WIDTH * 4 + QUAT * QUAT * 4
 
+VECTOR_SHARE = 64
+
 
 def tile_quaternionlinear_pa_v_kernel(tc, x, wr, wi, wj, wk, bias, grad_out, out_0, out_1):
     nc = tc.nc
-    x_rows = x.rearrange("b s w -> (b s) w").rearrange("(g p j) w -> g p j w", g=PASSES, j=PACK)
-    g_rows = grad_out.rearrange("b s w -> (b s) w").rearrange("(g p j) w -> g p j w", g=PASSES, j=PACK)
-    dx_rows = out_0.rearrange("b s w -> (b s) w").rearrange("(g p j) w -> g p j w", g=PASSES, j=PACK)
+
+    def by_token_tile(ap):
+        return ap.rearrange("b s w -> (b s) w").rearrange("(g p j) w -> g p j w", g=PASSES, j=PACK)
+
+    x_rows, g_rows, dx_rows = by_token_tile(x), by_token_tile(grad_out), by_token_tile(out_0)
     weights = (wr, wi, wj, wk)
 
     with ExitStack() as ctx:
@@ -44,12 +51,23 @@ def tile_quaternionlinear_pa_v_kernel(tc, x, wr, wi, wj, wk, bias, grad_out, out
         make_identity(nc, ident[:])
 
         g_raw = [keep.tile([P, PACK * WIDTH], BF16, name="g_raw%d" % g, align_bytes=64) for g in range(PASSES)]
-        x_raw = [keep.tile([P, PACK * QUAT], BF16, name="x_raw%d" % n, align_bytes=64) for n in range(PASSES * QTILES)]
+        x_raw = [keep.tile([P, PACK * QUAT], BF16, name="x_raw%d" % n, align_bytes=64) for n in range(X_CHUNKS)]
         w_raw = [keep.tile([P, PACK * QUAT], BF16, name="w_raw%d" % c, align_bytes=64) for c in range(COMP)]
         w_codes = [keep.tile([P, QUAT], U32, name="w_codes%d" % c, align_bytes=64) for c in range(COMP)]
         w_scales = [keep.tile([P, QUAT], U8, name="w_scales%d" % c, align_bytes=64) for c in range(COMP)]
         x_codes = [keep.tile([P, WIDTH], U32, name="x_codes%d" % g, align_bytes=64) for g in range(PASSES)]
         x_scales = [keep.tile([P, WIDTH], U8, name="x_scales%d" % g, align_bytes=64) for g in range(PASSES)]
+
+        grouped = {}
+        g_by_token = {}
+        presorted = {}
+        turned = {}
+        g_by_feature = {}
+        h_by_feature = {}
+        g_quantized = {}
+        h_quantized = {}
+        accs = {}
+        planar = {}
 
         def load_g(k):
             g, j = divmod(k, PACK)
@@ -66,19 +84,17 @@ def tile_quaternionlinear_pa_v_kernel(tc, x, wr, wi, wj, wk, bias, grad_out, out
         def copy_on(engine, out, in_):
             if engine == "vector":
                 nc.vector.tensor_copy(out=out, in_=in_)
-            elif engine == "gpsimd":
-                nc.gpsimd.tensor_scalar(out=out, in0=in_, scalar1=1.0, scalar2=0.0, op0=MULT, op1=ADD)
-            else:
+            elif engine == "scalar":
                 nc.scalar.copy(out=out, in_=in_)
+            else:
+                nc.gpsimd.tensor_scalar(out=out, in0=in_, scalar1=1.0, scalar2=0.0, op0=MULT, op1=ADD)
 
-        grouped = {}
-
-        def group_tile(owner):
+        def grouping_buffer(owner):
             depth = {"vector": 2, "scalar": 3, "gpsimd": 1}[owner]
             return work.tile([P, WIDTH], BF16, name="grp_" + owner, tag="grp_" + owner, bufs=depth, align_bytes=64)
 
         def group_weight(c, engine, owner):
-            t = group_tile(owner)
+            t = grouping_buffer(owner)
             copy_on(engine,
                     t[:].rearrange("p (b i j) -> p b j i", i=4, j=PACK),
                     w_raw[c][:].rearrange("p (j b i) -> p b j i", j=PACK, i=4))
@@ -88,33 +104,31 @@ def tile_quaternionlinear_pa_v_kernel(tc, x, wr, wi, wj, wk, bias, grad_out, out
             nc.vector.quantize_mx(out=w_codes[c][:].bitcast(E4M3), scales=w_scales[c][:], in_=grouped[("w", c)][:])
 
         def chunk_place(n):
-            if n < PASSES * QTILES:
+            if n < X_CHUNKS:
                 return divmod(n, QTILES)
-            q, g = divmod(n - PASSES * QTILES, PASSES)
+            q, g = divmod(n - X_CHUNKS, PASSES)
             return g, q
 
-        def group_chunk(n, engine):
+        def group_chunk(n, engine, owner, first, stop):
             g, q = chunk_place(n)
-            t = group_tile(engine)
-            if n < PASSES * QTILES:
+            if n not in grouped:
+                grouped[n] = grouping_buffer(owner)
+            t = grouped[n]
+            if n < X_CHUNKS:
                 raw = x_raw[n][:].rearrange("p (j w) -> p j w", j=PACK)
             else:
                 raw = g_raw[g][:].rearrange("p (j w) -> p j w", j=PACK)[:, :, q * QUAT:(q + 1) * QUAT]
             if engine == "gpsimd":
-                nc.gpsimd.tensor_scalar(out=t[:].rearrange("p (c i j) -> p i c j", c=COMP, j=PACK),
-                                        in0=raw.rearrange("p j (i c) -> p i c j", c=COMP),
-                                        scalar1=1.0, scalar2=0.0, op0=MULT, op1=ADD)
+                copy_on(engine, t[:].rearrange("p (c i j) -> p i j c", c=COMP, j=PACK)[:, first:stop],
+                        raw.rearrange("p j (i c) -> p i j c", c=COMP)[:, first:stop])
             else:
-                copy_on(engine, t[:].rearrange("p (c b i j) -> p b j i c", c=COMP, i=2, j=PACK),
-                        raw.rearrange("p j (b i c) -> p b j i c", i=2, c=COMP))
-            grouped[n] = t
-
-        gtok = {}
+                copy_on(engine, t[:].rearrange("p (c i a b) -> p i a c b", c=COMP, a=2, b=2)[:, first:stop],
+                        raw.rearrange("p (a b) (i c) -> p i a c b", a=2, c=COMP)[:, first:stop])
 
         def quantize_chunk(n):
             g, q = chunk_place(n)
             t = grouped[n]
-            if n < PASSES * QTILES:
+            if n < X_CHUNKS:
                 for c in range(COMP):
                     cols = slice(c * QUAT + q * P, c * QUAT + (q + 1) * P)
                     nc.vector.quantize_mx(out=x_codes[g][:, cols].bitcast(E4M3), scales=x_scales[g][:, cols],
@@ -123,46 +137,46 @@ def tile_quaternionlinear_pa_v_kernel(tc, x, wr, wi, wj, wk, bias, grad_out, out
                 codes = work.tile([P, QUAT], U32, name="gtok_codes", tag="gtok_codes", bufs=4, align_bytes=64)
                 scales = work.tile([P, QUAT], U8, name="gtok_scales", tag="gtok_scales", bufs=4, align_bytes=64)
                 nc.vector.quantize_mx(out=codes[:].bitcast(E5M2), scales=scales[:], in_=t[:])
-                gtok[(g, q)] = (codes, scales)
+                g_by_token[(g, q)] = (codes, scales)
 
-        banks = {}
+        def presort(k):
+            t = work.tile([P, WORDS], F32, name="sorted", tag="sorted", bufs=1)
+            words = g_raw[0][:].bitcast(F32)[:, k * WORDS:(k + 1) * WORDS]
+            nc.vector.tensor_copy(out=t[:].rearrange("p (t m h) -> p t m h", t=PACK, h=2),
+                                  in_=words.rearrange("p (m t h) -> p t m h", t=PACK, h=2))
+            presorted[k] = t
 
-        def transpose_tile(k):
+        def transpose_half(k, half):
             g, j = divmod(k, PACK)
             words = g_raw[g][:].bitcast(F32)
-            row = WIDTH // 2
-            for half in range(2):
-                bank = psum.tile([P, PACK * P], F32, name="turned", tag="turned")
-                for t in range(PACK):
-                    nc.tensor.transpose(bank[:, t * P:(t + 1) * P],
-                                        words[:, j * row + 2 * t + half:(j + 1) * row:8], ident[:])
-                banks[(k, half)] = bank[:].bitcast(BF16).rearrange("m (t p e) -> m e p t", t=PACK, e=2)
-
-        g_feat = {}
+            bank = psum.tile([P, PACK * P], F32, name="turned", tag="turned")
+            for t in range(PACK):
+                if k in presorted:
+                    columns = presorted[k][:, 2 * P * t + half:2 * P * (t + 1):2]
+                else:
+                    columns = words[:, j * WORDS + 2 * t + half:(j + 1) * WORDS:2 * PACK]
+                nc.tensor.transpose(bank[:, t * P:(t + 1) * P], columns, ident[:])
+            turned[(k, half)] = bank[:].bitcast(BF16).rearrange("m (t p e) -> m e p t", t=PACK, e=2)
 
         def copy_turned(k):
             t = work.tile([P, WIDTH], BF16, name="g_feat", tag="g_feat", align_bytes=64)
             for half in range(2):
-                nc.scalar.copy(out=t[:, half * 2 * QUAT:(half + 1) * 2 * QUAT].rearrange("m (e p t) -> m e p t", e=2, t=PACK),
-                               in_=banks[(k, half)])
-            g_feat[k] = t
-
-        gq = {}
-        hq = {}
-        h_feat = {}
+                part = t[:, half * 2 * QUAT:(half + 1) * 2 * QUAT]
+                nc.scalar.copy(out=part.rearrange("m (e p t) -> m e p t", e=2, t=PACK), in_=turned[(k, half)])
+            g_by_feature[k] = t
 
         def quantize_g(k):
             codes = work.tile([P, QUAT], U32, name="g_codes", tag="g_codes", align_bytes=64)
             scales = work.tile([P, QUAT], U8, name="g_scales", tag="g_scales", align_bytes=64)
-            nc.vector.quantize_mx(out=codes[:].bitcast(E5M2), scales=scales[:], in_=g_feat[k][:])
-            gq[k] = (codes, scales)
+            nc.vector.quantize_mx(out=codes[:].bitcast(E5M2), scales=scales[:], in_=g_by_feature[k][:])
+            g_quantized[k] = (codes, scales)
 
-        def combine(k):
+        def compute_h(k):
             sums = work.tile([P, 3 * QUAT], F32, name="sums", tag="sums", bufs=1)
             h = work.tile([P, 3 * QUAT], BF16, name="h_feat", tag="h_feat", align_bytes=64)
-            g0 = g_feat[k][:, 0:QUAT].rearrange("m (p t) -> m p t", t=PACK)
-            g1 = banks[(k, 0)][:, 1]
-            g23 = banks[(k, 1)]
+            g0 = g_by_feature[k][:, 0:QUAT].rearrange("m (p t) -> m p t", t=PACK)
+            g1 = turned[(k, 0)][:, 1]
+            g23 = turned[(k, 1)]
 
             def one(tile, s):
                 return tile[:, s * QUAT:(s + 1) * QUAT].rearrange("m (p t) -> m p t", t=PACK)
@@ -174,153 +188,151 @@ def tile_quaternionlinear_pa_v_kernel(tc, x, wr, wi, wj, wk, bias, grad_out, out
             nc.vector.tensor_tensor(out=one(sums, 2), in0=g1, in1=g0, op=ADD)
             nc.vector.tensor_tensor(out=one(h, 0), in0=g1, in1=one(sums, 0), op=SUB)
             nc.vector.tensor_tensor(out=two(h, 1), in0=g23, in1=two(sums, 1), op=SUB)
-            h_feat[k] = h
+            h_by_feature[k] = h
 
         def quantize_h(k):
             codes = work.tile([P, 3 * P], U32, name="h_codes", tag="h_codes", align_bytes=64)
             scales = work.tile([P, 3 * P], U8, name="h_scales", tag="h_scales", align_bytes=64)
-            h = h_feat[k]
+            h = h_by_feature[k]
             nc.vector.quantize_mx(out=codes[:, 0:2 * P].bitcast(E5M2), scales=scales[:, 0:2 * P], in_=h[:, 0:2 * QUAT])
             nc.vector.quantize_mx(out=codes[:, 2 * P:3 * P].bitcast(E5M2), scales=scales[:, 2 * P:3 * P],
                                   in_=h[:, 2 * QUAT:3 * QUAT])
-            hq[k] = (codes, scales)
+            h_quantized[k] = (codes, scales)
 
-        def mx(acc, left, s, right_codes, right_scales, start, stop):
+        def multiply(acc, left, s, right_codes, right_scales, start, stop):
             codes, scales = left
             cols = slice(s * P, (s + 1) * P)
             nc.tensor.matmul_mx(out=acc[:], lhsT=codes[:, cols].bitcast(E5M2), lhsT_scale=scales[:, cols],
                                 rhs=right_codes.bitcast(E4M3), rhs_scale=right_scales, start=start, stop=stop)
 
-        accs = {}
-
         def multiply_real(k):
             acc = psum.tile([P, QUAT], F32, name="acc", tag="acc")
             for c in range(COMP):
-                mx(acc, gq[k], c, w_codes[c][:], w_scales[c][:], c == 0, c == COMP - 1)
+                multiply(acc, g_quantized[k], c, w_codes[c][:], w_scales[c][:], c == 0, c == COMP - 1)
             accs[(k, 0)] = acc
 
         def open_imag(k, c):
             acc = psum.tile([P, QUAT], F32, name="acc", tag="acc")
-            mx(acc, gq[k], c, w_codes[0][:], w_scales[0][:], True, False)
+            multiply(acc, g_quantized[k], c, w_codes[0][:], w_scales[0][:], True, False)
             accs[(k, c)] = acc
 
         def close_imag(k, c):
-            mx(accs[(k, c)], hq[k], c % 3, w_codes[c][:], w_scales[c][:], False, True)
+            multiply(accs[(k, c)], h_quantized[k], c % 3, w_codes[c][:], w_scales[c][:], False, True)
 
         def multiply_weight_grad(q, g):
             if g == 0:
-                tag = "acc" if q < 2 else "turned"
+                tag = "acc" if q < QTILES - 2 else "turned"
                 accs[("w", q)] = psum.tile([P, QUAT], F32, name=tag, tag=tag)
             for c in range(COMP):
                 cols = slice(c * QUAT, (c + 1) * QUAT)
-                mx(accs[("w", q)], gtok[(g, q)], c, x_codes[g][:, cols], x_scales[g][:, cols],
-                   g == 0 and c == 0, g == PASSES - 1 and c == COMP - 1)
-
-        planar = {}
+                multiply(accs[("w", q)], g_by_token[(g, q)], c, x_codes[g][:, cols], x_scales[g][:, cols],
+                         g == 0 and c == 0, g == PASSES - 1 and c == COMP - 1)
 
         def drain(k, c, engine):
             if k not in planar:
                 planar[k] = work.tile([P, WIDTH], F32, name="planar", tag="planar")
             copy_on(engine, planar[k][:, c * QUAT:(c + 1) * QUAT], accs[(k, c)][:])
 
-        def drain_weight_grad(q, engine):
+        def drain_weight_grad(q):
             t = work.tile([P, QUAT], F32, name="dw", tag="dw")
-            copy_on(engine, t[:], accs[("w", q)][:])
+            nc.scalar.copy(out=t[:], in_=accs[("w", q)][:])
             nc.sync.dma_start(out=out_1[q * P:(q + 1) * P, :], in_=t[:])
 
         def weave_and_store(k, engines):
             g, j = divmod(k, PACK)
             t = work.tile([P, WIDTH], F32, name="woven", tag="woven", bufs=3)
-            dst = t[:].rearrange("p (b i c) -> p b c i", i=4, c=COMP)
-            src = planar[k][:].rearrange("p (c b i) -> p b c i", c=COMP, i=4)
-            nb = P // len(engines)
-            w = WIDTH // len(engines)
+            dst = t[:].rearrange("p (b i a e) -> p b a i e", i=2, a=2, e=2)
+            src = planar[k][:].rearrange("p (a e b i) -> p b a i e", a=2, e=2, i=2)
+            pairs = QUAT // 2 // len(engines)
+            width = WIDTH // len(engines)
             for s, engine in enumerate(engines):
-                copy_on(engine, dst[:, s * nb:(s + 1) * nb], src[:, s * nb:(s + 1) * nb])
-                nc.sync.dma_start(out=dx_rows[g, :, j, s * w:(s + 1) * w], in_=t[:, s * w:(s + 1) * w])
+                copy_on(engine, dst[:, s * pairs:(s + 1) * pairs], src[:, s * pairs:(s + 1) * pairs])
+                nc.sync.dma_start(out=dx_rows[g, :, j, s * width:(s + 1) * width], in_=t[:, s * width:(s + 1) * width])
 
         load_w(0)
-        load_w(1)
         load_g(0)
-        load_w(2)
-        load_w(3)
+        for c in range(1, COMP):
+            load_w(c)
         load_g(1)
         for n in range(3):
             load_x(n)
         for k in range(2, TILES):
             load_g(k)
-            for n in range(2 * k - 1, min(2 * k + 1, PASSES * QTILES)):
+            for n in range(2 * k - 1, min(2 * k + 1, X_CHUNKS)):
                 load_x(n)
 
         group_weight(0, "vector", "vector")
-        group_weight(1, "scalar", "scalar")
+        presort(0)
         quantize_weight(0)
-        transpose_tile(0)
+        transpose_half(0, 0)
+        transpose_half(0, 1)
         copy_turned(0)
+        group_weight(1, "vector", "vector")
         group_weight(2, "vector", "gpsimd")
         quantize_weight(1)
-        group_weight(3, "vector", "vector")
-        transpose_tile(1)
+        group_weight(3, "scalar", "scalar")
+        transpose_half(1, 0)
+        transpose_half(1, 1)
 
         last = TILES - 1
-        imag = (3, 2, 1)
-        scalar_chunks = [[1, 2], [4], [6], [8], [10], [12], [], [14]]
+        scalar_chunks = [[1, 2]] + [[2 * k + 2] for k in range(1, last - 1)] + [[], [2 * last]]
         for k in range(TILES):
-            q = k - 5
+            q = k - (TILES - QTILES + 1)
             quantize_g(k)
             if k == 0:
-                quantize_weight(3)
                 quantize_weight(2)
-                multiply_real(0)
             else:
                 multiply_real(k)
-                for c in imag:
+                for c in IMAG:
                     drain(k - 1, c, "scalar")
-                pass
                 quantize_chunk(2 * k - 1 if k > 1 else 0)
-            group_chunk(2 * k + 1 if k > 0 else 0, "gpsimd")
+            group_chunk(2 * k + 1 if k > 0 else 0, "gpsimd", "gpsimd", 0, P)
             if q >= 0:
                 for g in range(PASSES):
                     multiply_weight_grad(q, g)
             if k == last:
-                for c in imag:
+                for c in IMAG:
                     open_imag(k, c)
-            combine(k)
-            pass
+            compute_h(k)
+            if k == 0:
+                quantize_weight(3)
+                multiply_real(0)
             if k + 2 < TILES:
-                transpose_tile(k + 2)
+                transpose_half(k + 2, 0)
+            if k < last:
+                for c in IMAG[:2]:
+                    open_imag(k, c)
+            if 0 < k < TILES - 2:
+                transpose_half(k + 2, 1)
             if k < last:
                 copy_turned(k + 1)
-            if k == last and False:
-                quantize_chunk(15)
-                pass
-            if 0 < k < TILES and not (k == last and False):
-                weave_and_store(k - 1, ["vector"] if k < last else ["vector", "vector"])
+            if k == 0:
+                group_chunk(2, "vector", "scalar", 0, VECTOR_SHARE)
+            elif k < last:
+                weave_and_store(k - 1, ["vector"])
+            else:
+                weave_and_store(k - 1, ["scalar", "vector", "vector", "vector"])
             for n in scalar_chunks[k]:
-                group_chunk(n, "scalar")
+                group_chunk(n, "scalar", "scalar", VECTOR_SHARE if n == 2 else 0, P)
             drain(k, 0, "scalar")
             if q >= 0:
-                drain_weight_grad(q, "scalar")
-            if k == last - 1 and False:
-                for c in imag:
-                    open_imag(k, c)
+                drain_weight_grad(q)
             quantize_h(k)
-            for c in imag:
-                if k < last - 0:
+            for c in IMAG:
+                if (k, c) not in accs:
                     open_imag(k, c)
                 close_imag(k, c)
-            if k == last and False:
-                weave_and_store(k - 1, ["vector", "vector"])
-            if k > 0:
+            if k == 0:
+                transpose_half(2, 1)
+            else:
                 for n in scalar_chunks[k - 1]:
                     quantize_chunk(n)
 
-        quantize_chunk(14)
-        multiply_weight_grad(3, 0)
-        quantize_chunk(15)
-        multiply_weight_grad(3, 1)
+        for g in range(PASSES):
+            quantize_chunk(2 * last + g)
+            multiply_weight_grad(QTILES - 1, g)
         drain(last, 3, "scalar")
         drain(last, 2, "vector")
         drain(last, 1, "scalar")
         weave_and_store(last, ["vector", "vector", "scalar", "vector"])
-        drain_weight_grad(QTILES - 1, "scalar")
+        drain_weight_grad(QTILES - 1)

@@ -30,6 +30,7 @@ FLOPS = 2 * TOKENS * QUAT * QUAT * 14
 BYTES = 2 * TOKENS * WIDTH * 2 + 4 * QUAT * QUAT * 2 + TOKENS * WIDTH * 4 + QUAT * QUAT * 4
 
 VECTOR_SHARE = 64
+GPSIMD_SHARE = 8
 
 
 def tile_quaternionlinear_pa_v_kernel(tc, x, wr, wi, wj, wk, bias, grad_out, out_0, out_1):
@@ -287,6 +288,8 @@ def tile_quaternionlinear_pa_v_kernel(tc, x, wr, wi, wj, wk, bias, grad_out, out
                     drain(k - 1, c, "scalar")
                 quantize_chunk(2 * k - 1 if k > 1 else 0)
             group_chunk(2 * k + 1 if k > 0 else 0, "gpsimd", "gpsimd", 0, P)
+            if 0 < k < last:
+                group_chunk(2 * k + 2, "gpsimd", "scalar", 0, GPSIMD_SHARE)
             if q >= 0:
                 for g in range(PASSES):
                     multiply_weight_grad(q, g)
@@ -313,7 +316,7 @@ def tile_quaternionlinear_pa_v_kernel(tc, x, wr, wi, wj, wk, bias, grad_out, out
             else:
                 weave_and_store(k - 1, ["scalar", "vector", "vector", "vector"])
             for n in scalar_chunks[k]:
-                group_chunk(n, "scalar", "scalar", VECTOR_SHARE if n == 2 else 0, P)
+                group_chunk(n, "scalar", "scalar", {1: 0, 2: VECTOR_SHARE}.get(n, GPSIMD_SHARE), P)
             drain(k, 0, "scalar")
             if q >= 0:
                 drain_weight_grad(q)

from contextlib import ExitStack

import concourse.mybir as mybir
from concourse.masks import make_identity

F32 = mybir.dt.float32
BF16 = mybir.dt.bfloat16
U32 = mybir.dt.uint32
U8 = mybir.dt.uint8
E4M3 = mybir.dt.float8_e4m3fn_x4
E5M2 = mybir.dt.float8_e5m2_x4
ADD = mybir.AluOpType.add
SUB = mybir.AluOpType.subtract
MULT = mybir.AluOpType.mult

P = 128
PACK = 4
COMP = 4
TOKENS = 1024
QUAT = 512
WIDTH = QUAT * COMP
WORDS = WIDTH // 2
PASSES = TOKENS // (P * PACK)
TILES = PASSES * PACK
QTILES = QUAT // P
X_CHUNKS = PASSES * QTILES
IMAG = (3, 2, 1)

FLOPS = 2 * TOKENS * QUAT * QUAT * 14
BYTES = 2 * TOKENS * WIDTH * 2 + 4 * QUAT * QUAT * 2 + TOKENS * WIDTH * 4 + QUAT * QUAT * 4

VECTOR_SHARE = 64
GPSIMD_SHARE = 8


def tile_quaternionlinear_pa_v_kernel(tc, x, wr, wi, wj, wk, bias, grad_out, out_0, out_1):
    nc = tc.nc

    def by_token_tile(ap):
        return ap.rearrange("b s w -> (b s) w").rearrange("(g p j) w -> g p j w", g=PASSES, j=PACK)

    x_rows, g_rows, dx_rows = by_token_tile(x), by_token_tile(grad_out), by_token_tile(out_0)
    weights = (wr, wi, wj, wk)

    with ExitStack() as ctx:
        keep = ctx.enter_context(tc.tile_pool(name="keep", bufs=1))
        work = ctx.enter_context(tc.tile_pool(name="work", bufs=2))
        psum = ctx.enter_context(tc.psum_pool(name="psum", bufs=4))
        ctx.enter_context(tc.manual_schedule())

        ident = keep.tile([P, P], F32, name="ident")
        make_identity(nc, ident[:])

        g_raw = [keep.tile([P, PACK * WIDTH], BF16, name="g_raw%d" % g, align_bytes=64) for g in range(PASSES)]
        x_raw = [keep.tile([P, PACK * QUAT], BF16, name="x_raw%d" % n, align_bytes=64) for n in range(X_CHUNKS)]
        w_raw = [keep.tile([P, PACK * QUAT], BF16, name="w_raw%d" % c, align_bytes=64) for c in range(COMP)]
        w_codes = [keep.tile([P, QUAT], U32, name="w_codes%d" % c, align_bytes=64) for c in range(COMP)]
        w_scales = [keep.tile([P, QUAT], U8, name="w_scales%d" % c, align_bytes=64) for c in range(COMP)]
        x_codes = [keep.tile([P, WIDTH], U32, name="x_codes%d" % g, align_bytes=64) for g in range(PASSES)]
        x_scales = [keep.tile([P, WIDTH], U8, name="x_scales%d" % g, align_bytes=64) for g in range(PASSES)]

        grouped = {}
        g_by_token = {}
        presorted = {}
        turned = {}
        g_by_feature = {}
        h_by_feature = {}
        g_quantized = {}
        h_quantized = {}
        accs = {}
        planar = {}

        def load_g(k):
            g, j = divmod(k, PACK)
            nc.sync.dma_start(out=g_raw[g][:, j * WIDTH:(j + 1) * WIDTH], in_=g_rows[g, :, j, :])

        def load_w(c):
            nc.sync.dma_start(out=w_raw[c][:], in_=weights[c].rearrange("(p j) i -> p (j i)", j=PACK))

        def load_x(n):
            g, q = divmod(n, QTILES)
            nc.sync.dma_start(out=x_raw[n][:].rearrange("p (j w) -> p j w", j=PACK),
                              in_=x_rows[g, :, :, q * QUAT:(q + 1) * QUAT])

        def copy_on(engine, out, in_):
            if engine == "vector":
                nc.vector.tensor_copy(out=out, in_=in_)
            elif engine == "scalar":
                nc.scalar.copy(out=out, in_=in_)
            else:
                nc.gpsimd.tensor_scalar(out=out, in0=in_, scalar1=1.0, scalar2=0.0, op0=MULT, op1=ADD)

        def grouping_buffer(owner):
            depth = {"vector": 2, "scalar": 3, "gpsimd": 1}[owner]
            return work.tile([P, WIDTH], BF16, name="grp_" + owner, tag="grp_" + owner, bufs=depth, align_bytes=64)

        def group_weight(c, engine, owner):
            t = grouping_buffer(owner)
            copy_on(engine,
                    t[:].rearrange("p (b i j) -> p b j i", i=4, j=PACK),
                    w_raw[c][:].rearrange("p (j b i) -> p b j i", j=PACK, i=4))
            grouped[("w", c)] = t

        def quantize_weight(c):
            nc.vector.quantize_mx(out=w_codes[c][:].bitcast(E4M3), scales=w_scales[c][:], in_=grouped[("w", c)][:])

        def chunk_place(n):
            if n < X_CHUNKS:
                return divmod(n, QTILES)
            q, g = divmod(n - X_CHUNKS, PASSES)
            return g, q

        def group_chunk(n, engine, owner, first, stop):
            g, q = chunk_place(n)
            if n not in grouped:
                grouped[n] = grouping_buffer(owner)
            t = grouped[n]
            if n < X_CHUNKS:
                raw = x_raw[n][:].rearrange("p (j w) -> p j w", j=PACK)
            else:
                raw = g_raw[g][:].rearrange("p (j w) -> p j w", j=PACK)[:, :, q * QUAT:(q + 1) * QUAT]
            if engine == "gpsimd":
                copy_on(engine, t[:].rearrange("p (c i j) -> p i j c", c=COMP, j=PACK)[:, first:stop],
                        raw.rearrange("p j (i c) -> p i j c", c=COMP)[:, first:stop])
            else:
                copy_on(engine, t[:].rearrange("p (c i a b) -> p i a c b", c=COMP, a=2, b=2)[:, first:stop],
                        raw.rearrange("p (a b) (i c) -> p i a c b", a=2, c=COMP)[:, first:stop])

        def quantize_chunk(n):
            g, q = chunk_place(n)
            t = grouped[n]
            if n < X_CHUNKS:
                for c in range(COMP):
                    cols = slice(c * QUAT + q * P, c * QUAT + (q + 1) * P)
                    nc.vector.quantize_mx(out=x_codes[g][:, cols].bitcast(E4M3), scales=x_scales[g][:, cols],
                                          in_=t[:, c * QUAT:(c + 1) * QUAT])
            else:
                codes = work.tile([P, QUAT], U32, name="gtok_codes", tag="gtok_codes", bufs=4, align_bytes=64)
                scales = work.tile([P, QUAT], U8, name="gtok_scales", tag="gtok_scales", bufs=4, align_bytes=64)
                nc.vector.quantize_mx(out=codes[:].bitcast(E5M2), scales=scales[:], in_=t[:])
                g_by_token[(g, q)] = (codes, scales)

        def presort(k):
            t = work.tile([P, WORDS], F32, name="sorted", tag="sorted", bufs=1)
            words = g_raw[0][:].bitcast(F32)[:, k * WORDS:(k + 1) * WORDS]
            nc.vector.tensor_copy(out=t[:].rearrange("p (t m h) -> p t m h", t=PACK, h=2),
                                  in_=words.rearrange("p (m t h) -> p t m h", t=PACK, h=2))
            presorted[k] = t

        def transpose_half(k, half):
            g, j = divmod(k, PACK)
            words = g_raw[g][:].bitcast(F32)
            bank = psum.tile([P, PACK * P], F32, name="turned", tag="turned")
            for t in range(PACK):
                if k in presorted:
                    columns = presorted[k][:, 2 * P * t + half:2 * P * (t + 1):2]
                else:
                    columns = words[:, j * WORDS + 2 * t + half:(j + 1) * WORDS:2 * PACK]
                nc.tensor.transpose(bank[:, t * P:(t + 1) * P], columns, ident[:])
            turned[(k, half)] = bank[:].bitcast(BF16).rearrange("m (t p e) -> m e p t", t=PACK, e=2)

        def copy_turned(k):
            t = work.tile([P, WIDTH], BF16, name="g_feat", tag="g_feat", align_bytes=64)
            for half in range(2):
                part = t[:, half * 2 * QUAT:(half + 1) * 2 * QUAT]
                nc.scalar.copy(out=part.rearrange("m (e p t) -> m e p t", e=2, t=PACK), in_=turned[(k, half)])
            g_by_feature[k] = t

        def quantize_g(k):
            codes = work.tile([P, QUAT], U32, name="g_codes", tag="g_codes", align_bytes=64)
            scales = work.tile([P, QUAT], U8, name="g_scales", tag="g_scales", align_bytes=64)
            nc.vector.quantize_mx(out=codes[:].bitcast(E5M2), scales=scales[:], in_=g_by_feature[k][:])
            g_quantized[k] = (codes, scales)

        def compute_h(k):
            sums = work.tile([P, 3 * QUAT], F32, name="sums", tag="sums", bufs=1)
            h = work.tile([P, 3 * QUAT], BF16, name="h_feat", tag="h_feat", align_bytes=64)
            g0 = g_by_feature[k][:, 0:QUAT].rearrange("m (p t) -> m p t", t=PACK)
            g1 = turned[(k, 0)][:, 1]
            g23 = turned[(k, 1)]

            def one(tile, s):
                return tile[:, s * QUAT:(s + 1) * QUAT].rearrange("m (p t) -> m p t", t=PACK)

            def two(tile, s):
                return tile[:, s * QUAT:(s + 2) * QUAT].rearrange("m (e p t) -> m e p t", e=2, t=PACK)

            nc.vector.tensor_tensor(out=two(sums, 0), in0=g23, in1=g0.unsqueeze(1).to_broadcast([P, 2, P, PACK]), op=ADD)
            nc.vector.tensor_tensor(out=one(sums, 2), in0=g1, in1=g0, op=ADD)
            nc.vector.tensor_tensor(out=one(h, 0), in0=g1, in1=one(sums, 0), op=SUB)
            nc.vector.tensor_tensor(out=two(h, 1), in0=g23, in1=two(sums, 1), op=SUB)
            h_by_feature[k] = h

        def quantize_h(k):
            codes = work.tile([P, 3 * P], U32, name="h_codes", tag="h_codes", align_bytes=64)
            scales = work.tile([P, 3 * P], U8, name="h_scales", tag="h_scales", align_bytes=64)
            h = h_by_feature[k]
            nc.vector.quantize_mx(out=codes[:, 0:2 * P].bitcast(E5M2), scales=scales[:, 0:2 * P], in_=h[:, 0:2 * QUAT])
            nc.vector.quantize_mx(out=codes[:, 2 * P:3 * P].bitcast(E5M2), scales=scales[:, 2 * P:3 * P],
                                  in_=h[:, 2 * QUAT:3 * QUAT])
            h_quantized[k] = (codes, scales)

        def multiply(acc, left, s, right_codes, right_scales, start, stop):
            codes, scales = left
            cols = slice(s * P, (s + 1) * P)
            nc.tensor.matmul_mx(out=acc[:], lhsT=codes[:, cols].bitcast(E5M2), lhsT_scale=scales[:, cols],
                                rhs=right_codes.bitcast(E4M3), rhs_scale=right_scales, start=start, stop=stop)

        def multiply_real(k):
            acc = psum.tile([P, QUAT], F32, name="acc", tag="acc")
            for c in range(COMP):
                multiply(acc, g_quantized[k], c, w_codes[c][:], w_scales[c][:], c == 0, c == COMP - 1)
            accs[(k, 0)] = acc

        def open_imag(k, c):
            acc = psum.tile([P, QUAT], F32, name="acc", tag="acc")
            multiply(acc, g_quantized[k], c, w_codes[0][:], w_scales[0][:], True, False)
            accs[(k, c)] = acc

        def close_imag(k, c):
            multiply(accs[(k, c)], h_quantized[k], c % 3, w_codes[c][:], w_scales[c][:], False, True)

        def multiply_weight_grad(q, g):
            if g == 0:
                tag = "acc" if q < QTILES - 2 else "turned"
                accs[("w", q)] = psum.tile([P, QUAT], F32, name=tag, tag=tag)
            for c in range(COMP):
                cols = slice(c * QUAT, (c + 1) * QUAT)
                multiply(accs[("w", q)], g_by_token[(g, q)], c, x_codes[g][:, cols], x_scales[g][:, cols],
                         g == 0 and c == 0, g == PASSES - 1 and c == COMP - 1)

        def drain(k, c, engine):
            if k not in planar:
                planar[k] = work.tile([P, WIDTH], F32, name="planar", tag="planar")
            copy_on(engine, planar[k][:, c * QUAT:(c + 1) * QUAT], accs[(k, c)][:])

        def drain_weight_grad(q):
            t = work.tile([P, QUAT], F32, name="dw", tag="dw")
            nc.scalar.copy(out=t[:], in_=accs[("w", q)][:])
            nc.sync.dma_start(out=out_1[q * P:(q + 1) * P, :], in_=t[:])

        def weave_and_store(k, engines):
            g, j = divmod(k, PACK)
            t = work.tile([P, WIDTH], F32, name="woven", tag="woven", bufs=3)
            dst = t[:].rearrange("p (b i a e) -> p b a i e", i=2, a=2, e=2)
            src = planar[k][:].rearrange("p (a e b i) -> p b a i e", a=2, e=2, i=2)
            pairs = QUAT // 2 // len(engines)
            width = WIDTH // len(engines)
            for s, engine in enumerate(engines):
                copy_on(engine, dst[:, s * pairs:(s + 1) * pairs], src[:, s * pairs:(s + 1) * pairs])
                nc.sync.dma_start(out=dx_rows[g, :, j, s * width:(s + 1) * width], in_=t[:, s * width:(s + 1) * width])

        load_w(0)
        load_g(0)
        for c in range(1, COMP):
            load_w(c)
        load_g(1)
        for n in range(3):
            load_x(n)
        for k in range(2, TILES):
            load_g(k)
            for n in range(2 * k - 1, min(2 * k + 1, X_CHUNKS)):
                load_x(n)

        group_weight(0, "vector", "vector")
        presort(0)
        quantize_weight(0)
        transpose_half(0, 0)
        transpose_half(0, 1)
        copy_turned(0)
        group_weight(1, "vector", "vector")
        group_weight(2, "vector", "gpsimd")
        quantize_weight(1)
        group_weight(3, "scalar", "scalar")
        transpose_half(1, 0)
        transpose_half(1, 1)

        last = TILES - 1
        scalar_chunks = [[1, 2]] + [[2 * k + 2] for k in range(1, last - 1)] + [[], [2 * last]]
        for k in range(TILES):
            q = k - (TILES - QTILES + 1)
            quantize_g(k)
            if k == 0:
                quantize_weight(2)
            else:
                multiply_real(k)
                for c in IMAG:
                    drain(k - 1, c, "scalar")
                quantize_chunk(2 * k - 1 if k > 1 else 0)
            group_chunk(2 * k + 1 if k > 0 else 0, "gpsimd", "gpsimd", 0, P)
            if 0 < k < last:
                group_chunk(2 * k + 2, "gpsimd", "scalar", 0, GPSIMD_SHARE)
            if q >= 0:
                for g in range(PASSES):
                    multiply_weight_grad(q, g)
            if k == last:
                for c in IMAG:
                    open_imag(k, c)
            compute_h(k)
            if k == 0:
                quantize_weight(3)
                multiply_real(0)
            if k + 2 < TILES:
                transpose_half(k + 2, 0)
            if k < last:
                for c in IMAG[:2]:
                    open_imag(k, c)
            if 0 < k < TILES - 2:
                transpose_half(k + 2, 1)
            if k < last:
                copy_turned(k + 1)
            if k == 0:
                group_chunk(2, "vector", "scalar", 0, VECTOR_SHARE)
            elif k < last:
                weave_and_store(k - 1, ["vector"])
            else:
                weave_and_store(k - 1, ["scalar", "vector", "vector", "vector"])
            for n in scalar_chunks[k]:
                group_chunk(n, "scalar", "scalar", {1: 0, 2: VECTOR_SHARE}.get(n, GPSIMD_SHARE), P)
            drain(k, 0, "scalar")
            if q >= 0:
                drain_weight_grad(q)
            quantize_h(k)
            for c in IMAG:
                if (k, c) not in accs:
                    open_imag(k, c)
                close_imag(k, c)
            if k == 0:
                transpose_half(2, 1)
            else:
                for n in scalar_chunks[k - 1]:
                    quantize_chunk(n)

        for g in range(PASSES):
            quantize_chunk(2 * last + g)
            multiply_weight_grad(QTILES - 1, g)
        drain(last, 3, "scalar")
        drain(last, 2, "vector")
        drain(last, 1, "scalar")
        weave_and_store(last, ["vector", "vector", "scalar", "vector"])
        drain_weight_grad(QTILES - 1)
